import numpy as np
import ml_dtypes


def mxq(x, axis, fmt="e4m3"):
    dtype, down = {"e4m3": (ml_dtypes.float8_e4m3fn, 7), "e5m2": (ml_dtypes.float8_e5m2, 14)}[fmt]
    v = np.moveaxis(np.asarray(x, np.float32).astype(ml_dtypes.bfloat16).astype(np.float64), axis, -1)
    blocks = v.reshape(v.shape[:-1] + (-1, 32))
    amax = np.abs(blocks).max(-1, keepdims=True)
    byte = np.maximum(np.where(amax > 0, np.frexp(amax)[1] - 1 + 127, 0) - down, 1)
    scale = np.exp2(byte - 127.0)
    codes = (blocks / scale).astype(np.float32).astype(dtype).astype(np.float64)
    return np.moveaxis((codes * scale).reshape(v.shape), -1, axis)


WIDE = False


def mx_kscale(k):
    if not WIDE:
        return np.ones(k)
    levels = np.array([10, -10, 5, -5, 0])
    a = np.random.permutation(np.resize(levels, k // 512 * 4)).reshape(k // 512, 4)
    idx = np.arange(k)
    return np.exp2(a[idx // 512, idx % 128 // 32])


BF16 = ml_dtypes.bfloat16


def bf(x):
    return np.asarray(x, np.float32).astype(BF16)


def f64(x):
    return np.asarray(x).astype(np.float64)


B, C, H, W, ATT_DEPTH, PATCH = 1, 8, 512, 512, 1, 8
DS = 2 ** ATT_DEPTH
HS, WS = H // (PATCH * DS), W // (PATCH * DS)
HT, WT = H // PATCH, W // PATCH
LP, L, N = HS * WS, HT * WT, C * PATCH * PATCH


def setup_inputs():
    s = mx_kscale(LP)
    sx = np.repeat(np.repeat(s.reshape(HS, WS), PATCH * DS, axis=0), PATCH * DS, axis=1)
    x = np.random.standard_normal((B, C, H, W)) * 2.0 * DS / sx
    keep = 0.25 + 0.75 * np.random.random((B, 1, L, 1))
    keep = keep * (np.random.random((B, 1, L, 1)) >= 0.03)
    a = np.random.random((B, 1, L, LP)) * (np.random.random((B, 1, L, LP)) < keep)
    return {"x": bf(x), "attentions": bf(a * 0.3 * np.sqrt(LP) * s)}


def reference(x, attentions):
    x, attentions = f64(x), f64(attentions)
    argx = x.reshape(B, C, H // DS, DS, W // DS, DS).mean(axis=(3, 5))
    unf = argx.reshape(B, C, HS, PATCH, WS, PATCH).transpose(0, 1, 3, 5, 2, 4).reshape(B, N, LP)
    nz = np.where(attentions != 0.0, 1.0, 0.0).sum(axis=-1, keepdims=True) + 1e-05
    a = attentions / nz
    att = mxq(a, 3, "e4m3") @ mxq(unf[:, None].transpose(0, 1, 3, 2), 2, "e4m3")
    att = att[:, 0].transpose(0, 2, 1)
    return att.reshape(B, C, PATCH, PATCH, HT, WT).transpose(0, 1, 4, 2, 5, 3).reshape(B, C, H, W)

@@ -1,0 +1,228 @@
+from contextlib import ExitStack
+
+import concourse.mybir as mybir
+from concourse.masks import make_identity
+
+BF16 = mybir.dt.bfloat16
+F32 = mybir.dt.float32
+U32 = mybir.dt.uint32
+U8 = mybir.dt.uint8
+FP8X4 = mybir.dt.float8_e4m3fn_x4
+ALU = mybir.AluOpType
+ACT = mybir.ActivationFunctionType
+
+P = 128
+L = 4096
+LP = 1024
+N = 512
+FLOPS = 2 * L * LP * N
+
+NH = 2
+G = L // (P * NH)
+NB = 64 // G
+RC = 4
+NT = L // P
+NP = NT // 2
+PIN = False
+VSHARE = 3
+
+
+def tile_decode_atten_t_kernel(tc, x, attentions, out):
+    nc = tc.nc
+    with ExitStack() as ctx:
+        if PIN:
+            ctx.enter_context(tc.manual_schedule())
+        const = ctx.enter_context(tc.tile_pool(name="const", bufs=1))
+        xpool = ctx.enter_context(tc.tile_pool(name="xpool", bufs=4))
+        spool = ctx.enter_context(tc.tile_pool(name="spool", bufs=2))
+        apool = ctx.enter_context(tc.tile_pool(name="apool", bufs=6))
+        work = ctx.enter_context(tc.tile_pool(name="work", bufs=4))
+        jpool = ctx.enter_context(tc.tile_pool(name="jpool", bufs=2))
+        small = ctx.enter_context(tc.tile_pool(name="small", bufs=4))
+        cpool = ctx.enter_context(tc.tile_pool(name="cpool", bufs=3))
+        opool = ctx.enter_context(tc.tile_pool(name="opool", bufs=2))
+        psum_t = ctx.enter_context(tc.psum_pool(name="psum_t", bufs=4))
+        psum_o = ctx.enter_context(tc.psum_pool(name="psum_o", bufs=4))
+
+        ident = const.tile([P, P], BF16)
+        make_identity(nc, ident[:])
+        uq = const.tile([P, 2, N, 4], BF16, align_bytes=64)
+        ucodes = const.tile([P, 2, N], U32, align_bytes=64)
+        uscales = const.tile([P, 2, N], U8, align_bytes=64)
+
+        xv = x[0].rearrange("c (q a e k d) w -> e k (c q) a (d w)", q=8, a=4, e=2, k=4, d=2)
+        attv = attentions[0, 0].rearrange("(h p r) j -> h p r j", h=NH, p=P, r=G)
+        ov = out[0].rearrange("c (h lh kh) (b w) -> c h b lh kh w", h=NH, kh=8, b=NB)
+
+        xs = []
+        for k in range(4):
+            xs_k = xpool.tile([P, 4, 1024], BF16, name="xs")
+            for e in range(2):
+                nc.sync.dma_start(out=xs_k[e:P:2, :, :], in_=xv[e, k])
+            xs.append(xs_k)
+        chunks = []
+        for ci in range(NT // RC):
+            at_c = apool.tile([P, RC, LP], BF16, name="at_c")
+            h, r0 = divmod(ci * RC, G)
+            nc.sync.dma_start(out=at_c[:], in_=attv[h, :, r0 : r0 + RC, :])
+            chunks.append(at_c)
+
+        def row(t):
+            return chunks[t // RC][:, t % RC, :]
+
+        def pool_x(k):
+            s1 = spool.tile([P, 4, 512], F32, name="s1")
+            nc.vector.tensor_tensor(out=s1[:], in0=xs[k][:, :, 0:512], in1=xs[k][:, :, 512:1024], op=ALU.add)
+            g = work.tile([P, 1024], BF16, name="g")
+            s1v = s1[:].rearrange("p a (m d) -> p a m d", d=2)
+            nc.vector.tensor_tensor(
+                out=g[:].rearrange("p (a m) -> p a m", a=4),
+                in0=s1v[:, :, :, 0],
+                in1=s1v[:, :, :, 1],
+                op=ALU.add,
+            )
+            tp = psum_o.tile([P, 1024], BF16, name="mo")
+            gv = g[:].rearrange("p (m w) -> p m w", w=8)
+            for w in range(8):
+                nc.tensor.transpose(tp[:, w * P : (w + 1) * P], gv[:, :, w], ident[:])
+            tv = tp[:].rearrange("p (m s t e) -> p s m e t", m=64, s=2, t=4, e=2)
+            for s in range(2):
+                nc.scalar.activation(
+                    out=uq[:, s, k * P : (k + 1) * P, :].rearrange("p (m e) t -> p m e t", e=2),
+                    in_=tv[:, s],
+                    func=ACT.Copy,
+                    scale=0.25,
+                )
+
+        state = {}
+
+        def count(i):
+            nz = small.tile([P, 2], F32, name="nz")
+            for j in range(2):
+                junk = jpool.tile([P, LP], BF16, name="junk")
+                nc.vector.tensor_scalar(
+                    out=junk[:],
+                    in0=row(2 * i + j),
+                    scalar1=0.0,
+                    scalar2=1e-05,
+                    op0=ALU.not_equal,
+                    op1=ALU.add,
+                    accum_out=nz[:, j : j + 1],
+                )
+            rnz = small.tile([P, 2], F32, name="rnz")
+            nc.vector.reciprocal(out=rnz[:], in_=nz[:])
+            state[("rnz", i)] = rnz
+
+        def scale(i):
+            rnz = state[("rnz", i)]
+            tiles = []
+            for j in range(2):
+                a_t = work.tile([P, LP], BF16, name="a_t")
+                nc.vector.tensor_scalar(
+                    out=a_t[:], in0=row(2 * i + j), scalar1=rnz[:, j : j + 1], scalar2=None, op0=ALU.mult
+                )
+                tiles.append(a_t)
+            state[("a", i)] = tiles
+
+        def transpose(i):
+            banks = []
+            for j in range(2):
+                a_t = state[("a", i)][j]
+                tp = psum_t.tile([P, 1024], BF16, name="tp")
+                for b in range(8):
+                    nc.tensor.transpose(tp[:, b * P : (b + 1) * P], a_t[:, b * P : (b + 1) * P], ident[:])
+                banks.append(tp)
+            state[("tp", i)] = banks
+
+        def regroup(i):
+            grp = cpool.tile([P, 2, 2, P, 4], BF16, name="grp", align_bytes=64)
+            for j in range(2):
+                nc.scalar.copy(
+                    out=grp[:, j], in_=state[("tp", i)][j][:].rearrange("p (s t l) -> p s l t", s=2, t=4)
+                )
+            state[("grp", i)] = grp
+
+        def quantise(i):
+            codes = cpool.tile([P, 4 * P], U32, name="codes", align_bytes=64)
+            scl = cpool.tile([P, 4 * P], U8, name="scl", align_bytes=64)
+            nc.vector.quantize_mx(
+                out=codes[:].bitcast(FP8X4),
+                scales=scl[:],
+                in_=state[("grp", i)][:].rearrange("p j s l t -> p (j s l t)"),
+            )
+            state[("q", i)] = (codes, scl)
+
+        def multiply(i):
+            codes, scl = state[("q", i)]
+            banks = []
+            for j in range(2):
+                mo = psum_o.tile([P, N], F32, name="mo")
+                for s in range(2):
+                    c0 = (2 * j + s) * P
+                    nc.tensor.matmul_mx(
+                        out=mo[:],
+                        lhsT=codes[:, c0 : c0 + P].bitcast(FP8X4),
+                        lhsT_scale=scl[:, c0 : c0 + P],
+                        rhs=ucodes[:, s, :].bitcast(FP8X4),
+                        rhs_scale=uscales[:, s, :],
+                        start=(s == 0),
+                        stop=(s == 1),
+                    )
+                banks.append(mo)
+            state[("mo", i)] = banks
+
+        def store(h, stage, r0, r1):
+            for c in range(8):
+                for b in range(NB):
+                    nc.sync.dma_start(
+                        out=ov[c, h, b][:, :, r0 * 8 : r1 * 8],
+                        in_=stage[b:P:NB, c * 8 : (c + 1) * 8, r0:r1, :].rearrange("p kh r w -> p kh (r w)"),
+                    )
+
+        def empty(i):
+            for j in range(2):
+                t = 2 * i + j
+                h, r = divmod(t, G)
+                if r == 0:
+                    state["stage"] = opool.tile([P, 64, G, 8], F32, name="stage")
+                stage = state["stage"]
+                dst = stage[:, :, r, :].rearrange("p (m k) w -> p m k w", k=4)
+                src = state[("mo", i)][j][:].rearrange("p (k w m) -> p m k w", k=4, w=8, m=16)
+                if t % VSHARE == VSHARE - 1:
+                    nc.vector.tensor_copy(out=dst, in_=src)
+                else:
+                    nc.scalar.copy(out=dst, in_=src)
+                if h < NH - 1 and r == G - 1:
+                    store(h, stage, 0, G)
+                if h == NH - 1 and r == G // 2 - 1:
+                    store(h, stage, 0, G // 2)
+                if h == NH - 1 and r == G - 1:
+                    store(h, stage, G // 2, G)
+
+        def step(n):
+            if 0 <= n + 2 < NP:
+                count(n + 2)
+            if 0 <= n + 1 < NP:
+                transpose(n + 1)
+            if 0 <= n - 1 < NP:
+                empty(n - 1)
+            if 0 <= n < NP:
+                quantise(n)
+            if 0 <= n + 1 < NP:
+                regroup(n + 1)
+            if 0 <= n + 2 < NP:
+                scale(n + 2)
+            if 0 <= n < NP:
+                multiply(n)
+
+        for k in range(4):
+            pool_x(k)
+        step(-2)
+        step(-1)
+        nc.vector.quantize_mx(
+            out=ucodes[:].rearrange("p s n -> p (s n)").bitcast(FP8X4),
+            scales=uscales[:].rearrange("p s n -> p (s n)"),
+            in_=uq[:].rearrange("p s n t -> p (s n t)"),
+        )
+        for n in range(NP + 2):
+            step(n)

@@ -34,46 +34,82 @@ def tile_decode_atten_t_kernel(tc, x, attentions, out):
             ctx.enter_context(tc.manual_schedule())
         const = ctx.enter_context(tc.tile_pool(name="const", bufs=1))
         xpool = ctx.enter_context(tc.tile_pool(name="xpool", bufs=4))
-        spool = ctx.enter_context(tc.tile_pool(name="spool", bufs=2))
+        gpool = ctx.enter_context(tc.tile_pool(name="gpool", bufs=2))
         apool = ctx.enter_context(tc.tile_pool(name="apool", bufs=6))
         work = ctx.enter_context(tc.tile_pool(name="work", bufs=4))
         jpool = ctx.enter_context(tc.tile_pool(name="jpool", bufs=2))
         small = ctx.enter_context(tc.tile_pool(name="small", bufs=4))
-        cpool = ctx.enter_context(tc.tile_pool(name="cpool", bufs=3))
+        rpool = ctx.enter_context(tc.tile_pool(name="rpool", bufs=3))
+        qpool = ctx.enter_context(tc.tile_pool(name="qpool", bufs=6))
         opool = ctx.enter_context(tc.tile_pool(name="opool", bufs=2))
         psum_t = ctx.enter_context(tc.psum_pool(name="psum_t", bufs=4))
         psum_o = ctx.enter_context(tc.psum_pool(name="psum_o", bufs=4))
 
         ident = const.tile([P, P], BF16)
         make_identity(nc, ident[:])
+        pair = const.tile([P, 192], BF16)
+        nc.vector.memset(pair[:], 0.0)
+        idv = ident[:].rearrange("p (m d) -> p m d", d=2)
+        nc.vector.tensor_tensor(out=pair[:, 64:128], in0=idv[:, :, 0], in1=idv[:, :, 1], op=ALU.add)
         uq = const.tile([P, 2, N, 4], BF16, align_bytes=64)
         ucodes = const.tile([P, 2, N], U32, align_bytes=64)
         uscales = const.tile([P, 2, N], U8, align_bytes=64)
 
-        xv = x[0].rearrange("c (q a e k d) w -> e k (c q) a (d w)", q=8, a=4, e=2, k=4, d=2)
+        xva = x[0].rearrange("c (q a e k d) w -> e k (c q) a (d w)", q=8, a=4, e=2, k=4, d=2)
+        xvb = x[0].rearrange("(hh c) (q a e k d) w -> hh e k d (c q) a w", hh=2, c=4, q=8, a=4, e=2, k=4, d=2)
         attv = attentions[0, 0].rearrange("(h p r) j -> h p r j", h=NH, p=P, r=G)
         ov = out[0].rearrange("c (h lh kh) (b w) -> c h b lh kh w", h=NH, kh=8, b=NB)
 
-        xs = []
-        for k in range(4):
-            xs_k = xpool.tile([P, 4, 1024], BF16, name="xs")
-            for e in range(2):
-                nc.sync.dma_start(out=xs_k[e:P:2, :, :], in_=xv[e, k])
-            xs.append(xs_k)
-        chunks = []
-        for ci in range(NT // RC):
+        xs = {}
+        chunks = {}
+
+        def load_x(k):
+            if k == 0:
+                xs_k = xpool.tile([P, 4, 1024], BF16, name="xs")
+                for e in range(2):
+                    nc.sync.dma_start(out=xs_k[e:P:2, :, :], in_=xva[e, k])
+            else:
+                xs_k = xpool.tile([P, 2, 4, 512], BF16, name="xs")
+                for hh in range(2):
+                    for e in range(2):
+                        for d in range(2):
+                            nc.sync.dma_start(out=xs_k[2 * e + d : P : 4, hh, :, :], in_=xvb[hh, e, k, d])
+            xs[k] = xs_k
+
+        def load_att(ci):
             at_c = apool.tile([P, RC, LP], BF16, name="at_c")
             h, r0 = divmod(ci * RC, G)
             nc.sync.dma_start(out=at_c[:], in_=attv[h, :, r0 : r0 + RC, :])
-            chunks.append(at_c)
+            chunks[ci] = at_c
+
+        for item in [["x",0],["a",0],["x",1],["a",1],["x",2],["x",3],["a",2],["a",3],["a",4],["a",5],["a",6],["a",7]]:
+            if item[0] == "x":
+                load_x(item[1])
+            else:
+                load_att(item[1])
 
         def row(t):
             return chunks[t // RC][:, t % RC, :]
 
-        def pool_x(k):
-            s1 = spool.tile([P, 4, 512], F32, name="s1")
+        def finish_u(k, tp, scaled):
+            tv = tp[:].rearrange("p (m s t e) -> p s m e t", m=64, s=2, t=4, e=2)
+            for s in range(2):
+                dst = uq[:, s, k * P : (k + 1) * P, :].rearrange("p (m e) t -> p m e t", e=2)
+                if scaled:
+                    nc.scalar.copy(out=dst, in_=tv[:, s])
+                else:
+                    nc.scalar.activation(out=dst, in_=tv[:, s], func=ACT.Copy, scale=0.25)
+            for s in range(2):
+                nc.vector.quantize_mx(
+                    out=ucodes[:, s, k * P : (k + 1) * P].bitcast(FP8X4),
+                    scales=uscales[:, s, k * P : (k + 1) * P],
+                    in_=uq[:, s, k * P : (k + 1) * P, :].rearrange("p n t -> p (n t)"),
+                )
+
+        def pool_vector(k):
+            s1 = const.tile([P, 4, 512], F32, name="s1")
             nc.vector.tensor_tensor(out=s1[:], in0=xs[k][:, :, 0:512], in1=xs[k][:, :, 512:1024], op=ALU.add)
-            g = work.tile([P, 1024], BF16, name="g")
+            g = gpool.tile([P, 1024], BF16, name="g")
             s1v = s1[:].rearrange("p a (m d) -> p a m d", d=2)
             nc.vector.tensor_tensor(
                 out=g[:].rearrange("p (a m) -> p a m", a=4),
@@ -85,14 +121,34 @@ def tile_decode_atten_t_kernel(tc, x, attentions, out):
             gv = g[:].rearrange("p (m w) -> p m w", w=8)
             for w in range(8):
                 nc.tensor.transpose(tp[:, w * P : (w + 1) * P], gv[:, :, w], ident[:])
-            tv = tp[:].rearrange("p (m s t e) -> p s m e t", m=64, s=2, t=4, e=2)
-            for s in range(2):
+            finish_u(k, tp, False)
+
+        def pool_tensor(k):
+            gd = gpool.tile([P, 8, P], BF16, name="g")
+            for beta in range(2):
+                ps = psum_o.tile([P, 512], F32, name="mo")
+                idx = 0
+                for hh in range(2):
+                    cols = xs[k][:, hh, 2 * beta : 2 * beta + 2, :].rearrange("p a (m d) -> p (a m) d", d=2)
+                    for d in range(2):
+                        nc.tensor.matmul(
+                            out=ps[:],
+                            lhsT=pair[:, 64 - 64 * hh : 192 - 64 * hh],
+                            rhs=cols[:, :, d],
+                            start=(idx == 0),
+                            stop=(idx == 3),
+                        )
+                        idx += 1
                 nc.scalar.activation(
-                    out=uq[:, s, k * P : (k + 1) * P, :].rearrange("p (m e) t -> p m e t", e=2),
-                    in_=tv[:, s],
+                    out=gd[:, :, beta * 64 : (beta + 1) * 64],
+                    in_=ps[:].rearrange("p (m w) -> p w m", w=8),
                     func=ACT.Copy,
                     scale=0.25,
                 )
+            tp = psum_o.tile([P, 1024], BF16, name="mo")
+            for w in range(8):
+                nc.tensor.transpose(tp[:, w * P : (w + 1) * P], gd[:, w, :], ident[:])
+            finish_u(k, tp, True)
 
         state = {}
 
@@ -135,7 +191,7 @@ def tile_decode_atten_t_kernel(tc, x, attentions, out):
             state[("tp", i)] = banks
 
         def regroup(i):
-            grp = cpool.tile([P, 2, 2, P, 4], BF16, name="grp", align_bytes=64)
+            grp = rpool.tile([P, 2, 2, P, 4], BF16, name="grp", align_bytes=64)
             for j in range(2):
                 nc.scalar.copy(
                     out=grp[:, j], in_=state[("tp", i)][j][:].rearrange("p (s t l) -> p s l t", s=2, t=4)
@@ -143,8 +199,8 @@ def tile_decode_atten_t_kernel(tc, x, attentions, out):
             state[("grp", i)] = grp
 
         def quantise(i):
-            codes = cpool.tile([P, 4 * P], U32, name="codes", align_bytes=64)
-            scl = cpool.tile([P, 4 * P], U8, name="scl", align_bytes=64)
+            codes = qpool.tile([P, 4 * P], U32, name="codes", align_bytes=64)
+            scl = qpool.tile([P, 4 * P], U8, name="scl", align_bytes=64)
             nc.vector.quantize_mx(
                 out=codes[:].bitcast(FP8X4),
                 scales=scl[:],
@@ -199,30 +255,34 @@ def tile_decode_atten_t_kernel(tc, x, attentions, out):
                 if h == NH - 1 and r == G - 1:
                     store(h, stage, G // 2, G)
 
-        def step(n):
+        def step(n, emp, mult):
             if 0 <= n + 2 < NP:
                 count(n + 2)
             if 0 <= n + 1 < NP:
                 transpose(n + 1)
-            if 0 <= n - 1 < NP:
-                empty(n - 1)
+            for i in emp:
+                empty(i)
             if 0 <= n < NP:
                 quantise(n)
             if 0 <= n + 1 < NP:
                 regroup(n + 1)
             if 0 <= n + 2 < NP:
                 scale(n + 2)
-            if 0 <= n < NP:
-                multiply(n)
+            for i in mult:
+                multiply(i)
 
-        for k in range(4):
-            pool_x(k)
-        step(-2)
-        step(-1)
-        nc.vector.quantize_mx(
-            out=ucodes[:].rearrange("p s n -> p (s n)").bitcast(FP8X4),
-            scales=uscales[:].rearrange("p s n -> p (s n)"),
-            in_=uq[:].rearrange("p s n t -> p (s n t)"),
-        )
-        for n in range(NP + 2):
-            step(n)
+        pool_vector(0)
+        step(-2, [], [])
+        step(-1, [], [])
+        pool_tensor(1)
+        step(0, [], [])
+        pool_tensor(2)
+        step(1, [], [])
+        pool_tensor(3)
+        step(2, [], [])
+        step(3, [], [0, 1])
+        step(4, [0, 1], [2, 3])
+        step(5, [2, 3], [4, 5])
+        step(6, [4, 5], [6])
+        for n in range(7, NP + 1):
+            step(n, [n - 1], [n] if n < NP else [])

@@ -24,7 +24,7 @@ RC = 4
 NT = L // P
 NP = NT // 2
 PIN = False
-VSHARE = 3
+VSHARE = 1
 
 
 def tile_decode_atten_t_kernel(tc, x, attentions, out):
@@ -174,8 +174,13 @@ def tile_decode_atten_t_kernel(tc, x, attentions, out):
             tiles = []
             for j in range(2):
                 a_t = work.tile([P, LP], BF16, name="a_t")
-                nc.vector.tensor_scalar(
-                    out=a_t[:], in0=row(2 * i + j), scalar1=rnz[:, j : j + 1], scalar2=None, op0=ALU.mult
+                nc.gpsimd.tensor_scalar(
+                    out=a_t[:],
+                    in0=row(2 * i + j),
+                    scalar1=rnz[:, j : j + 1],
+                    scalar2=0.0,
+                    op0=ALU.mult,
+                    op1=ALU.add,
                 )
                 tiles.append(a_t)
             state[("a", i)] = tiles

@@ -23,8 +23,12 @@ NB = 64 // G
 RC = 4
 NT = L // P
 NP = NT // 2
-PIN = False
-VSHARE = 1
+PIN = True
+LM = 4
+M0 = 8
+CR = 3
+UQ = [1,5,7,8]
+PX = [0,2,4,5]
 
 
 def tile_decode_atten_t_kernel(tc, x, attentions, out):
@@ -40,7 +44,7 @@ def tile_decode_atten_t_kernel(tc, x, attentions, out):
         jpool = ctx.enter_context(tc.tile_pool(name="jpool", bufs=2))
         small = ctx.enter_context(tc.tile_pool(name="small", bufs=4))
         rpool = ctx.enter_context(tc.tile_pool(name="rpool", bufs=3))
-        qpool = ctx.enter_context(tc.tile_pool(name="qpool", bufs=6))
+        qpool = ctx.enter_context(tc.tile_pool(name="qpool", bufs=8))
         opool = ctx.enter_context(tc.tile_pool(name="opool", bufs=2))
         psum_t = ctx.enter_context(tc.psum_pool(name="psum_t", bufs=4))
         psum_o = ctx.enter_context(tc.psum_pool(name="psum_o", bufs=4))
@@ -91,14 +95,18 @@ def tile_decode_atten_t_kernel(tc, x, attentions, out):
         def row(t):
             return chunks[t // RC][:, t % RC, :]
 
-        def finish_u(k, tp, scaled):
-            tv = tp[:].rearrange("p (m s t e) -> p s m e t", m=64, s=2, t=4, e=2)
+        state = {}
+
+        def regroup_u(k, scaled):
+            tv = state[("tu", k)][:].rearrange("p (m s t e) -> p s m e t", m=64, s=2, t=4, e=2)
             for s in range(2):
                 dst = uq[:, s, k * P : (k + 1) * P, :].rearrange("p (m e) t -> p m e t", e=2)
                 if scaled:
                     nc.scalar.copy(out=dst, in_=tv[:, s])
                 else:
                     nc.scalar.activation(out=dst, in_=tv[:, s], func=ACT.Copy, scale=0.25)
+
+        def quantise_u(k):
             for s in range(2):
                 nc.vector.quantize_mx(
                     out=ucodes[:, s, k * P : (k + 1) * P].bitcast(FP8X4),
@@ -121,10 +129,10 @@ def tile_decode_atten_t_kernel(tc, x, attentions, out):
             gv = g[:].rearrange("p (m w) -> p m w", w=8)
             for w in range(8):
                 nc.tensor.transpose(tp[:, w * P : (w + 1) * P], gv[:, :, w], ident[:])
-            finish_u(k, tp, False)
+            state[("tu", k)] = tp
 
-        def pool_tensor(k):
-            gd = gpool.tile([P, 8, P], BF16, name="g")
+        def pool_matmuls(k):
+            banks = []
             for beta in range(2):
                 ps = psum_o.tile([P, 512], F32, name="mo")
                 idx = 0
@@ -139,18 +147,26 @@ def tile_decode_atten_t_kernel(tc, x, attentions, out):
                             stop=(idx == 3),
                         )
                         idx += 1
+                banks.append(ps)
+            state[("ps", k)] = banks
+
+        def round_g(k):
+            gd = gpool.tile([P, 8, P], BF16, name="g")
+            for beta in range(2):
                 nc.scalar.activation(
                     out=gd[:, :, beta * 64 : (beta + 1) * 64],
-                    in_=ps[:].rearrange("p (m w) -> p w m", w=8),
+                    in_=state[("ps", k)][beta][:].rearrange("p (m w) -> p w m", w=8),
                     func=ACT.Copy,
                     scale=0.25,
                 )
+            state[("gd", k)] = gd
+
+        def transpose_u(k):
+            gd = state[("gd", k)]
             tp = psum_o.tile([P, 1024], BF16, name="mo")
             for w in range(8):
                 nc.tensor.transpose(tp[:, w * P : (w + 1) * P], gd[:, w, :], ident[:])
-            finish_u(k, tp, True)
-
-        state = {}
+            state[("tu", k)] = tp
 
         def count(i):
             nz = small.tile([P, 2], F32, name="nz")
@@ -174,13 +190,8 @@ def tile_decode_atten_t_kernel(tc, x, attentions, out):
             tiles = []
             for j in range(2):
                 a_t = work.tile([P, LP], BF16, name="a_t")
-                nc.gpsimd.tensor_scalar(
-                    out=a_t[:],
-                    in0=row(2 * i + j),
-                    scalar1=rnz[:, j : j + 1],
-                    scalar2=0.0,
-                    op0=ALU.mult,
-                    op1=ALU.add,
+                nc.vector.tensor_scalar(
+                    out=a_t[:], in0=row(2 * i + j), scalar1=rnz[:, j : j + 1], scalar2=None, op0=ALU.mult
                 )
                 tiles.append(a_t)
             state[("a", i)] = tiles
@@ -212,7 +223,6 @@ def tile_decode_atten_t_kernel(tc, x, attentions, out):
                 in_=state[("grp", i)][:].rearrange("p j s l t -> p (j s l t)"),
             )
             state[("q", i)] = (codes, scl)
-
         def multiply(i):
             codes, scl = state[("q", i)]
             banks = []
@@ -232,6 +242,7 @@ def tile_decode_atten_t_kernel(tc, x, attentions, out):
                 banks.append(mo)
             state[("mo", i)] = banks
 
+
         def store(h, stage, r0, r1):
             for c in range(8):
                 for b in range(NB):
@@ -240,54 +251,68 @@ def tile_decode_atten_t_kernel(tc, x, attentions, out):
                         in_=stage[b:P:NB, c * 8 : (c + 1) * 8, r0:r1, :].rearrange("p kh r w -> p kh (r w)"),
                     )
 
-        def empty(i):
+        def on_vector(t):
+            return t % 2 == 1
+
+        def empty(i, vector):
             for j in range(2):
                 t = 2 * i + j
                 h, r = divmod(t, G)
-                if r == 0:
-                    state["stage"] = opool.tile([P, 64, G, 8], F32, name="stage")
-                stage = state["stage"]
+                if ("stage", h) not in state:
+                    state[("stage", h)] = opool.tile([P, 64, G, 8], F32, name="stage")
+                stage = state[("stage", h)]
                 dst = stage[:, :, r, :].rearrange("p (m k) w -> p m k w", k=4)
                 src = state[("mo", i)][j][:].rearrange("p (k w m) -> p m k w", k=4, w=8, m=16)
-                if t % VSHARE == VSHARE - 1:
+                if vector and on_vector(t):
                     nc.vector.tensor_copy(out=dst, in_=src)
-                else:
+                if not vector and not on_vector(t):
                     nc.scalar.copy(out=dst, in_=src)
-                if h < NH - 1 and r == G - 1:
-                    store(h, stage, 0, G)
-                if h == NH - 1 and r == G // 2 - 1:
-                    store(h, stage, 0, G // 2)
-                if h == NH - 1 and r == G - 1:
-                    store(h, stage, G // 2, G)
 
-        def step(n, emp, mult):
-            if 0 <= n + 2 < NP:
-                count(n + 2)
-            if 0 <= n + 1 < NP:
-                transpose(n + 1)
-            for i in emp:
-                empty(i)
-            if 0 <= n < NP:
-                quantise(n)
-            if 0 <= n + 1 < NP:
-                regroup(n + 1)
-            if 0 <= n + 2 < NP:
-                scale(n + 2)
-            for i in mult:
-                multiply(i)
+        def stores_after(i):
+            h, r = divmod(2 * i + 1, G)
+            stage = state[("stage", h)]
+            if h < NH - 1 and r == G - 1:
+                store(h, stage, 0, G)
+            if h == NH - 1 and r == G // 2 - 1:
+                store(h, stage, 0, G // 2)
+            if h == NH - 1 and r == G - 1:
+                store(h, stage, G // 2, G)
+
+        def m_step(i):
+            return max(i + LM, M0 + (i + CR - 1) // CR)
 
         pool_vector(0)
-        step(-2, [], [])
-        step(-1, [], [])
-        pool_tensor(1)
-        step(0, [], [])
-        pool_tensor(2)
-        step(1, [], [])
-        pool_tensor(3)
-        step(2, [], [])
-        step(3, [], [0, 1])
-        step(4, [0, 1], [2, 3])
-        step(5, [2, 3], [4, 5])
-        step(6, [4, 5], [6])
-        for n in range(7, NP + 1):
-            step(n, [n - 1], [n] if n < NP else [])
+        regroup_u(0, False)
+        for n in range(NP + LM + 1):
+            due = [i for i in range(NP) if m_step(i) == n]
+            for k in range(4):
+                if UQ[k] == n:
+                    quantise_u(k)
+            for i in due:
+                multiply(i)
+            for k in range(1, 4):
+                if PX[k] == n:
+                    pool_matmuls(k)
+            for k in range(1, 4):
+                if PX[k] + 1 == n:
+                    transpose_u(k)
+            if 0 <= n - 1 < NP:
+                transpose(n - 1)
+            for i in due:
+                empty(i, True)
+            if n < NP:
+                count(n)
+                scale(n)
+            if 0 <= n - 2 < NP:
+                quantise(n - 2)
+            for k in range(1, 4):
+                if PX[k] + 2 == n:
+                    regroup_u(k, True)
+            for i in due:
+                empty(i, False)
+                stores_after(i)
+            for k in range(1, 4):
+                if PX[k] == n:
+                    round_g(k)
+            if 0 <= n - 1 < NP:
+                regroup(n - 1)

@@ -196,21 +196,18 @@ def tile_decode_atten_t_kernel(tc, x, attentions, out):
                 tiles.append(a_t)
             state[("a", i)] = tiles
 
-        def transpose(i):
-            banks = []
-            for j in range(2):
-                a_t = state[("a", i)][j]
-                tp = psum_t.tile([P, 1024], BF16, name="tp")
-                for b in range(8):
-                    nc.tensor.transpose(tp[:, b * P : (b + 1) * P], a_t[:, b * P : (b + 1) * P], ident[:])
-                banks.append(tp)
-            state[("tp", i)] = banks
+        def transpose(t):
+            a_t = state[("a", t // 2)][t % 2]
+            tp = psum_t.tile([P, 1024], BF16, name="tp")
+            for b in range(8):
+                nc.tensor.transpose(tp[:, b * P : (b + 1) * P], a_t[:, b * P : (b + 1) * P], ident[:])
+            state[("tp", t)] = tp
 
         def regroup(i):
             grp = rpool.tile([P, 2, 2, P, 4], BF16, name="grp", align_bytes=64)
             for j in range(2):
                 nc.scalar.copy(
-                    out=grp[:, j], in_=state[("tp", i)][j][:].rearrange("p (s t l) -> p s l t", s=2, t=4)
+                    out=grp[:, j], in_=state[("tp", 2 * i + j)][:].rearrange("p (s t l) -> p s l t", s=2, t=4)
                 )
             state[("grp", i)] = grp
 
@@ -223,24 +220,21 @@ def tile_decode_atten_t_kernel(tc, x, attentions, out):
                 in_=state[("grp", i)][:].rearrange("p j s l t -> p (j s l t)"),
             )
             state[("q", i)] = (codes, scl)
-        def multiply(i):
-            codes, scl = state[("q", i)]
-            banks = []
-            for j in range(2):
-                mo = psum_o.tile([P, N], F32, name="mo")
-                for s in range(2):
-                    c0 = (2 * j + s) * P
-                    nc.tensor.matmul_mx(
-                        out=mo[:],
-                        lhsT=codes[:, c0 : c0 + P].bitcast(FP8X4),
-                        lhsT_scale=scl[:, c0 : c0 + P],
-                        rhs=ucodes[:, s, :].bitcast(FP8X4),
-                        rhs_scale=uscales[:, s, :],
-                        start=(s == 0),
-                        stop=(s == 1),
-                    )
-                banks.append(mo)
-            state[("mo", i)] = banks
+        def multiply(t):
+            codes, scl = state[("q", t // 2)]
+            mo = psum_o.tile([P, N], F32, name="mo")
+            for s in range(2):
+                c0 = (2 * (t % 2) + s) * P
+                nc.tensor.matmul_mx(
+                    out=mo[:],
+                    lhsT=codes[:, c0 : c0 + P].bitcast(FP8X4),
+                    lhsT_scale=scl[:, c0 : c0 + P],
+                    rhs=ucodes[:, s, :].bitcast(FP8X4),
+                    rhs_scale=uscales[:, s, :],
+                    start=(s == 0),
+                    stop=(s == 1),
+                )
+            state[("mo", t)] = mo
 
 
         def store(h, stage, r0, r1):
@@ -262,7 +256,7 @@ def tile_decode_atten_t_kernel(tc, x, attentions, out):
                     state[("stage", h)] = opool.tile([P, 64, G, 8], F32, name="stage")
                 stage = state[("stage", h)]
                 dst = stage[:, :, r, :].rearrange("p (m k) w -> p m k w", k=4)
-                src = state[("mo", i)][j][:].rearrange("p (k w m) -> p m k w", k=4, w=8, m=16)
+                src = state[("mo", t)][:].rearrange("p (k w m) -> p m k w", k=4, w=8, m=16)
                 if vector and on_vector(t):
                     nc.vector.tensor_copy(out=dst, in_=src)
                 if not vector and not on_vector(t):
@@ -288,16 +282,19 @@ def tile_decode_atten_t_kernel(tc, x, attentions, out):
             for k in range(4):
                 if UQ[k] == n:
                     quantise_u(k)
-            for i in due:
-                multiply(i)
+            mx_tiles = [2 * i + j for i in due for j in range(2)]
+            tr_tiles = [2 * (n - 1) + j for j in range(2) if 0 <= n - 1 < NP]
             for k in range(1, 4):
                 if PX[k] == n:
                     pool_matmuls(k)
             for k in range(1, 4):
                 if PX[k] + 1 == n:
                     transpose_u(k)
-            if 0 <= n - 1 < NP:
-                transpose(n - 1)
+            for idx in range(max(len(mx_tiles), len(tr_tiles))):
+                if idx < len(mx_tiles):
+                    multiply(mx_tiles[idx])
+                if idx < len(tr_tiles):
+                    transpose(tr_tiles[idx])
             for i in due:
                 empty(i, True)
             if n < NP:

@@ -196,18 +196,21 @@ def tile_decode_atten_t_kernel(tc, x, attentions, out):
                 tiles.append(a_t)
             state[("a", i)] = tiles
 
-        def transpose(t):
-            a_t = state[("a", t // 2)][t % 2]
-            tp = psum_t.tile([P, 1024], BF16, name="tp")
-            for b in range(8):
-                nc.tensor.transpose(tp[:, b * P : (b + 1) * P], a_t[:, b * P : (b + 1) * P], ident[:])
-            state[("tp", t)] = tp
+        def transpose(i):
+            banks = []
+            for j in range(2):
+                a_t = state[("a", i)][j]
+                tp = psum_t.tile([P, 1024], BF16, name="tp")
+                for b in range(8):
+                    nc.tensor.transpose(tp[:, b * P : (b + 1) * P], a_t[:, b * P : (b + 1) * P], ident[:])
+                banks.append(tp)
+            state[("tp", i)] = banks
 
         def regroup(i):
             grp = rpool.tile([P, 2, 2, P, 4], BF16, name="grp", align_bytes=64)
             for j in range(2):
                 nc.scalar.copy(
-                    out=grp[:, j], in_=state[("tp", 2 * i + j)][:].rearrange("p (s t l) -> p s l t", s=2, t=4)
+                    out=grp[:, j], in_=state[("tp", i)][j][:].rearrange("p (s t l) -> p s l t", s=2, t=4)
                 )
             state[("grp", i)] = grp
 
@@ -220,21 +223,24 @@ def tile_decode_atten_t_kernel(tc, x, attentions, out):
                 in_=state[("grp", i)][:].rearrange("p j s l t -> p (j s l t)"),
             )
             state[("q", i)] = (codes, scl)
-        def multiply(t):
-            codes, scl = state[("q", t // 2)]
-            mo = psum_o.tile([P, N], F32, name="mo")
-            for s in range(2):
-                c0 = (2 * (t % 2) + s) * P
-                nc.tensor.matmul_mx(
-                    out=mo[:],
-                    lhsT=codes[:, c0 : c0 + P].bitcast(FP8X4),
-                    lhsT_scale=scl[:, c0 : c0 + P],
-                    rhs=ucodes[:, s, :].bitcast(FP8X4),
-                    rhs_scale=uscales[:, s, :],
-                    start=(s == 0),
-                    stop=(s == 1),
-                )
-            state[("mo", t)] = mo
+        def multiply(i):
+            codes, scl = state[("q", i)]
+            banks = []
+            for j in range(2):
+                mo = psum_o.tile([P, N], F32, name="mo")
+                for s in range(2):
+                    c0 = (2 * j + s) * P
+                    nc.tensor.matmul_mx(
+                        out=mo[:],
+                        lhsT=codes[:, c0 : c0 + P].bitcast(FP8X4),
+                        lhsT_scale=scl[:, c0 : c0 + P],
+                        rhs=ucodes[:, s, :].bitcast(FP8X4),
+                        rhs_scale=uscales[:, s, :],
+                        start=(s == 0),
+                        stop=(s == 1),
+                    )
+                banks.append(mo)
+            state[("mo", i)] = banks
 
 
         def store(h, stage, r0, r1):
@@ -256,7 +262,7 @@ def tile_decode_atten_t_kernel(tc, x, attentions, out):
                     state[("stage", h)] = opool.tile([P, 64, G, 8], F32, name="stage")
                 stage = state[("stage", h)]
                 dst = stage[:, :, r, :].rearrange("p (m k) w -> p m k w", k=4)
-                src = state[("mo", t)][:].rearrange("p (k w m) -> p m k w", k=4, w=8, m=16)
+                src = state[("mo", i)][j][:].rearrange("p (k w m) -> p m k w", k=4, w=8, m=16)
                 if vector and on_vector(t):
                     nc.vector.tensor_copy(out=dst, in_=src)
                 if not vector and not on_vector(t):
@@ -265,11 +271,9 @@ def tile_decode_atten_t_kernel(tc, x, attentions, out):
         def stores_after(i):
             h, r = divmod(2 * i + 1, G)
             stage = state[("stage", h)]
-            if h < NH - 1 and r == G - 1:
-                store(h, stage, 0, G)
-            if h == NH - 1 and r == G // 2 - 1:
+            if r == G // 2 - 1:
                 store(h, stage, 0, G // 2)
-            if h == NH - 1 and r == G - 1:
+            if r == G - 1:
                 store(h, stage, G // 2, G)
 
         def m_step(i):
@@ -282,19 +286,16 @@ def tile_decode_atten_t_kernel(tc, x, attentions, out):
             for k in range(4):
                 if UQ[k] == n:
                     quantise_u(k)
-            mx_tiles = [2 * i + j for i in due for j in range(2)]
-            tr_tiles = [2 * (n - 1) + j for j in range(2) if 0 <= n - 1 < NP]
+            for i in due:
+                multiply(i)
             for k in range(1, 4):
                 if PX[k] == n:
                     pool_matmuls(k)
             for k in range(1, 4):
                 if PX[k] + 1 == n:
                     transpose_u(k)
-            for idx in range(max(len(mx_tiles), len(tr_tiles))):
-                if idx < len(mx_tiles):
-                    multiply(mx_tiles[idx])
-                if idx < len(tr_tiles):
-                    transpose(tr_tiles[idx])
+            if 0 <= n - 1 < NP:
+                transpose(n - 1)
             for i in due:
                 empty(i, True)
             if n < NP:

@@ -199,11 +199,13 @@ def tile_decode_atten_t_kernel(tc, x, attentions, out):
         def transpose(i):
             banks = []
             for j in range(2):
-                a_t = state[("a", i)][j]
                 tp = psum_t.tile([P, 1024], BF16, name="tp")
-                for b in range(8):
-                    nc.tensor.transpose(tp[:, b * P : (b + 1) * P], a_t[:, b * P : (b + 1) * P], ident[:])
                 banks.append(tp)
+            for half in range(2):
+                for j in range(2):
+                    a_t = state[("a", i)][j]
+                    for b in range(4 * half, 4 * half + 4):
+                        nc.tensor.transpose(banks[j][:, b * P : (b + 1) * P], a_t[:, b * P : (b + 1) * P], ident[:])
             state[("tp", i)] = banks
 
         def regroup(i):

from contextlib import ExitStack

import concourse.mybir as mybir
from concourse.masks import make_identity

BF16 = mybir.dt.bfloat16
F32 = mybir.dt.float32
U32 = mybir.dt.uint32
U8 = mybir.dt.uint8
FP8X4 = mybir.dt.float8_e4m3fn_x4
ALU = mybir.AluOpType
ACT = mybir.ActivationFunctionType

P = 128
L = 4096
LP = 1024
N = 512
FLOPS = 2 * L * LP * N

NH = 2
G = L // (P * NH)
NB = 64 // G
RC = 4
NT = L // P
NP = NT // 2
PIN = True
LM = 4
M0 = 8
CR = 3
UQ = [1,5,7,8]
PX = [0,2,4,5]


def tile_decode_atten_t_kernel(tc, x, attentions, out):
    nc = tc.nc
    with ExitStack() as ctx:
        if PIN:
            ctx.enter_context(tc.manual_schedule())
        const = ctx.enter_context(tc.tile_pool(name="const", bufs=1))
        xpool = ctx.enter_context(tc.tile_pool(name="xpool", bufs=4))
        gpool = ctx.enter_context(tc.tile_pool(name="gpool", bufs=2))
        apool = ctx.enter_context(tc.tile_pool(name="apool", bufs=6))
        work = ctx.enter_context(tc.tile_pool(name="work", bufs=4))
        jpool = ctx.enter_context(tc.tile_pool(name="jpool", bufs=2))
        small = ctx.enter_context(tc.tile_pool(name="small", bufs=4))
        rpool = ctx.enter_context(tc.tile_pool(name="rpool", bufs=3))
        qpool = ctx.enter_context(tc.tile_pool(name="qpool", bufs=8))
        opool = ctx.enter_context(tc.tile_pool(name="opool", bufs=2))
        psum_t = ctx.enter_context(tc.psum_pool(name="psum_t", bufs=4))
        psum_o = ctx.enter_context(tc.psum_pool(name="psum_o", bufs=4))

        ident = const.tile([P, P], BF16)
        make_identity(nc, ident[:])
        pair = const.tile([P, 192], BF16)
        nc.vector.memset(pair[:], 0.0)
        idv = ident[:].rearrange("p (m d) -> p m d", d=2)
        nc.vector.tensor_tensor(out=pair[:, 64:128], in0=idv[:, :, 0], in1=idv[:, :, 1], op=ALU.add)
        uq = const.tile([P, 2, N, 4], BF16, align_bytes=64)
        ucodes = const.tile([P, 2, N], U32, align_bytes=64)
        uscales = const.tile([P, 2, N], U8, align_bytes=64)

        xva = x[0].rearrange("c (q a e k d) w -> e k (c q) a (d w)", q=8, a=4, e=2, k=4, d=2)
        xvb = x[0].rearrange("(hh c) (q a e k d) w -> hh e k d (c q) a w", hh=2, c=4, q=8, a=4, e=2, k=4, d=2)
        attv = attentions[0, 0].rearrange("(h p r) j -> h p r j", h=NH, p=P, r=G)
        ov = out[0].rearrange("c (h lh kh) (b w) -> c h b lh kh w", h=NH, kh=8, b=NB)

        xs = {}
        chunks = {}

        def load_x(k):
            if k == 0:
                xs_k = xpool.tile([P, 4, 1024], BF16, name="xs")
                for e in range(2):
                    nc.sync.dma_start(out=xs_k[e:P:2, :, :], in_=xva[e, k])
            else:
                xs_k = xpool.tile([P, 2, 4, 512], BF16, name="xs")
                for hh in range(2):
                    for e in range(2):
                        for d in range(2):
                            nc.sync.dma_start(out=xs_k[2 * e + d : P : 4, hh, :, :], in_=xvb[hh, e, k, d])
            xs[k] = xs_k

        def load_att(ci):
            at_c = apool.tile([P, RC, LP], BF16, name="at_c")
            h, r0 = divmod(ci * RC, G)
            nc.sync.dma_start(out=at_c[:], in_=attv[h, :, r0 : r0 + RC, :])
            chunks[ci] = at_c

        for item in [["x",0],["a",0],["x",1],["a",1],["x",2],["x",3],["a",2],["a",3],["a",4],["a",5],["a",6],["a",7]]:
            if item[0] == "x":
                load_x(item[1])
            else:
                load_att(item[1])

        def row(t):
            return chunks[t // RC][:, t % RC, :]

        state = {}

        def regroup_u(k, scaled):
            tv = state[("tu", k)][:].rearrange("p (m s t e) -> p s m e t", m=64, s=2, t=4, e=2)
            for s in range(2):
                dst = uq[:, s, k * P : (k + 1) * P, :].rearrange("p (m e) t -> p m e t", e=2)
                if scaled:
                    nc.scalar.copy(out=dst, in_=tv[:, s])
                else:
                    nc.scalar.activation(out=dst, in_=tv[:, s], func=ACT.Copy, scale=0.25)

        def quantise_u(k):
            for s in range(2):
                nc.vector.quantize_mx(
                    out=ucodes[:, s, k * P : (k + 1) * P].bitcast(FP8X4),
                    scales=uscales[:, s, k * P : (k + 1) * P],
                    in_=uq[:, s, k * P : (k + 1) * P, :].rearrange("p n t -> p (n t)"),
                )

        def pool_vector(k):
            s1 = const.tile([P, 4, 512], F32, name="s1")
            nc.vector.tensor_tensor(out=s1[:], in0=xs[k][:, :, 0:512], in1=xs[k][:, :, 512:1024], op=ALU.add)
            g = gpool.tile([P, 1024], BF16, name="g")
            s1v = s1[:].rearrange("p a (m d) -> p a m d", d=2)
            nc.vector.tensor_tensor(
                out=g[:].rearrange("p (a m) -> p a m", a=4),
                in0=s1v[:, :, :, 0],
                in1=s1v[:, :, :, 1],
                op=ALU.add,
            )
            tp = psum_o.tile([P, 1024], BF16, name="mo")
            gv = g[:].rearrange("p (m w) -> p m w", w=8)
            for w in range(8):
                nc.tensor.transpose(tp[:, w * P : (w + 1) * P], gv[:, :, w], ident[:])
            state[("tu", k)] = tp

        def pool_matmuls(k):
            banks = []
            for beta in range(2):
                ps = psum_o.tile([P, 512], F32, name="mo")
                idx = 0
                for hh in range(2):
                    cols = xs[k][:, hh, 2 * beta : 2 * beta + 2, :].rearrange("p a (m d) -> p (a m) d", d=2)
                    for d in range(2):
                        nc.tensor.matmul(
                            out=ps[:],
                            lhsT=pair[:, 64 - 64 * hh : 192 - 64 * hh],
                            rhs=cols[:, :, d],
                            start=(idx == 0),
                            stop=(idx == 3),
                        )
                        idx += 1
                banks.append(ps)
            state[("ps", k)] = banks

        def round_g(k):
            gd = gpool.tile([P, 8, P], BF16, name="g")
            for beta in range(2):
                nc.scalar.activation(
                    out=gd[:, :, beta * 64 : (beta + 1) * 64],
                    in_=state[("ps", k)][beta][:].rearrange("p (m w) -> p w m", w=8),
                    func=ACT.Copy,
                    scale=0.25,
                )
            state[("gd", k)] = gd

        def transpose_u(k):
            gd = state[("gd", k)]
            tp = psum_o.tile([P, 1024], BF16, name="mo")
            for w in range(8):
                nc.tensor.transpose(tp[:, w * P : (w + 1) * P], gd[:, w, :], ident[:])
            state[("tu", k)] = tp

        def count(i):
            nz = small.tile([P, 2], F32, name="nz")
            for j in range(2):
                junk = jpool.tile([P, LP], BF16, name="junk")
                nc.vector.tensor_scalar(
                    out=junk[:],
                    in0=row(2 * i + j),
                    scalar1=0.0,
                    scalar2=1e-05,
                    op0=ALU.not_equal,
                    op1=ALU.add,
                    accum_out=nz[:, j : j + 1],
                )
            rnz = small.tile([P, 2], F32, name="rnz")
            nc.vector.reciprocal(out=rnz[:], in_=nz[:])
            state[("rnz", i)] = rnz

        def scale(i):
            rnz = state[("rnz", i)]
            tiles = []
            for j in range(2):
                a_t = work.tile([P, LP], BF16, name="a_t")
                nc.vector.tensor_scalar(
                    out=a_t[:], in0=row(2 * i + j), scalar1=rnz[:, j : j + 1], scalar2=None, op0=ALU.mult
                )
                tiles.append(a_t)
            state[("a", i)] = tiles

        def transpose(i):
            banks = []
            for j in range(2):
                tp = psum_t.tile([P, 1024], BF16, name="tp")
                banks.append(tp)
            for half in range(2):
                for j in range(2):
                    a_t = state[("a", i)][j]
                    for b in range(4 * half, 4 * half + 4):
                        nc.tensor.transpose(banks[j][:, b * P : (b + 1) * P], a_t[:, b * P : (b + 1) * P], ident[:])
            state[("tp", i)] = banks

        def regroup(i):
            grp = rpool.tile([P, 2, 2, P, 4], BF16, name="grp", align_bytes=64)
            for j in range(2):
                nc.scalar.copy(
                    out=grp[:, j], in_=state[("tp", i)][j][:].rearrange("p (s t l) -> p s l t", s=2, t=4)
                )
            state[("grp", i)] = grp

        def quantise(i):
            codes = qpool.tile([P, 4 * P], U32, name="codes", align_bytes=64)
            scl = qpool.tile([P, 4 * P], U8, name="scl", align_bytes=64)
            nc.vector.quantize_mx(
                out=codes[:].bitcast(FP8X4),
                scales=scl[:],
                in_=state[("grp", i)][:].rearrange("p j s l t -> p (j s l t)"),
            )
            state[("q", i)] = (codes, scl)
        def multiply(i):
            codes, scl = state[("q", i)]
            banks = []
            for j in range(2):
                mo = psum_o.tile([P, N], F32, name="mo")
                for s in range(2):
                    c0 = (2 * j + s) * P
                    nc.tensor.matmul_mx(
                        out=mo[:],
                        lhsT=codes[:, c0 : c0 + P].bitcast(FP8X4),
                        lhsT_scale=scl[:, c0 : c0 + P],
                        rhs=ucodes[:, s, :].bitcast(FP8X4),
                        rhs_scale=uscales[:, s, :],
                        start=(s == 0),
                        stop=(s == 1),
                    )
                banks.append(mo)
            state[("mo", i)] = banks


        def store(h, stage, r0, r1):
            for c in range(8):
                for b in range(NB):
                    nc.sync.dma_start(
                        out=ov[c, h, b][:, :, r0 * 8 : r1 * 8],
                        in_=stage[b:P:NB, c * 8 : (c + 1) * 8, r0:r1, :].rearrange("p kh r w -> p kh (r w)"),
                    )

        def on_vector(t):
            return t % 2 == 1

        def empty(i, vector):
            for j in range(2):
                t = 2 * i + j
                h, r = divmod(t, G)
                if ("stage", h) not in state:
                    state[("stage", h)] = opool.tile([P, 64, G, 8], F32, name="stage")
                stage = state[("stage", h)]
                dst = stage[:, :, r, :].rearrange("p (m k) w -> p m k w", k=4)
                src = state[("mo", i)][j][:].rearrange("p (k w m) -> p m k w", k=4, w=8, m=16)
                if vector and on_vector(t):
                    nc.vector.tensor_copy(out=dst, in_=src)
                if not vector and not on_vector(t):
                    nc.scalar.copy(out=dst, in_=src)

        def stores_after(i):
            h, r = divmod(2 * i + 1, G)
            stage = state[("stage", h)]
            if r == G // 2 - 1:
                store(h, stage, 0, G // 2)
            if r == G - 1:
                store(h, stage, G // 2, G)

        def m_step(i):
            return max(i + LM, M0 + (i + CR - 1) // CR)

        pool_vector(0)
        regroup_u(0, False)
        for n in range(NP + LM + 1):
            due = [i for i in range(NP) if m_step(i) == n]
            for k in range(4):
                if UQ[k] == n:
                    quantise_u(k)
            for i in due:
                multiply(i)
            for k in range(1, 4):
                if PX[k] == n:
                    pool_matmuls(k)
            for k in range(1, 4):
                if PX[k] + 1 == n:
                    transpose_u(k)
            if 0 <= n - 1 < NP:
                transpose(n - 1)
            for i in due:
                empty(i, True)
            if n < NP:
                count(n)
                scale(n)
            if 0 <= n - 2 < NP:
                quantise(n - 2)
            for k in range(1, 4):
                if PX[k] + 2 == n:
                    regroup_u(k, True)
            for i in due:
                empty(i, False)
                stores_after(i)
            for k in range(1, 4):
                if PX[k] == n:
                    round_g(k)
            if 0 <= n - 1 < NP:
                regroup(n - 1)
